import numpy as np
import ml_dtypes


def mxq(x, axis, fmt="e4m3"):
    dtype, down = {"e4m3": (ml_dtypes.float8_e4m3fn, 7), "e5m2": (ml_dtypes.float8_e5m2, 14)}[fmt]
    v = np.moveaxis(np.asarray(x, np.float32).astype(ml_dtypes.bfloat16).astype(np.float64), axis, -1)
    blocks = v.reshape(v.shape[:-1] + (-1, 32))
    amax = np.abs(blocks).max(-1, keepdims=True)
    byte = np.maximum(np.where(amax > 0, np.frexp(amax)[1] - 1 + 127, 0) - down, 1)
    scale = np.exp2(byte - 127.0)
    codes = (blocks / scale).astype(np.float32).astype(dtype).astype(np.float64)
    return np.moveaxis((codes * scale).reshape(v.shape), -1, axis)


WIDE = False


def mx_kscale(k):
    if not WIDE:
        return np.ones(k)
    levels = np.array([10, -10, 5, -5, 0])
    a = np.random.permutation(np.resize(levels, k // 512 * 4)).reshape(k // 512, 4)
    idx = np.arange(k)
    return np.exp2(a[idx // 512, idx % 128 // 32])


BF16 = ml_dtypes.bfloat16


def bf(x):
    return np.asarray(x, np.float32).astype(BF16)


def f64(x):
    return np.asarray(x).astype(np.float64)


B, H, L, D = 8, 2, 512, 512
NEG = -100.0


def setup_inputs():
    s = mx_kscale(D)
    return {"q": bf(np.random.standard_normal((B, H, L, D)) * s),
            "e": bf(np.random.standard_normal((H, L, D)) / np.sqrt(D) / s)}


def reference(q, e):
    rel = mxq(f64(q), 3, "e4m3") @ mxq(f64(e), 2, "e4m3").transpose(0, 2, 1)
    rel = rel.reshape(B * H, L, L)
    rel = np.pad(rel, ((0, 0), (0, 0), (1, 0)), constant_values=NEG)
    rel = rel.reshape(B * H, L + 1, L)[:, 1:, :][:, :L, :]
    mask = np.triu(np.ones((L, L), dtype=bool), k=1)
    rel = np.where(mask[None, :, :], 0.0, rel)
    return rel.reshape(B, H, L, L)

@@ -1,0 +1,194 @@
+from contextlib import ExitStack
+
+import concourse.mybir as mybir
+from concourse.masks import make_identity
+
+F32 = mybir.dt.float32
+BF16 = mybir.dt.bfloat16
+U32 = mybir.dt.uint32
+U8 = mybir.dt.uint8
+FP8X4 = mybir.dt.float8_e4m3fn_x4
+MULT = mybir.AluOpType.mult
+IS_GE = mybir.AluOpType.is_ge
+
+B, H, L, D = 8, 2, 512, 512
+P = 128
+ROWS = 8
+RUN = ROWS * (L + 1)
+NB = 4
+NA = P // NB
+FLOPS = 2 * B * H * L * L * D
+
+
+def tile_subsampledrelativeattention_t_kernel(tc, q, e, out):
+    nc = tc.nc
+    out_flat = out.rearrange("b h i j -> (b h i j)")
+    groups = [(h, nq, g) for g in range(2) for h in range(H) for nq in range(2)]
+
+    with ExitStack() as ctx:
+        const = ctx.enter_context(tc.tile_pool(name="const", bufs=1))
+        raw_pool = ctx.enter_context(tc.tile_pool(name="raw", bufs=8))
+        stage_pool = ctx.enter_context(tc.tile_pool(name="stage", bufs=2))
+        code_pool = ctx.enter_context(tc.tile_pool(name="code", bufs=3))
+        out_pool = ctx.enter_context(tc.tile_pool(name="outp", bufs=1))
+        psum_t = ctx.enter_context(tc.psum_pool(name="psum_t", bufs=3))
+        psum_m = ctx.enter_context(tc.psum_pool(name="psum_m", bufs=5))
+
+        e_raw = raw_pool.tile([P, 4096], BF16, tag="raw", name="e_raw")
+
+        def load_e(h):
+            nc.sync.dma_start(
+                out=e_raw[:, 2048 * h : 2048 * (h + 1)].rearrange("p (t d) -> p t d", t=4),
+                in_=e[h].rearrange("(t p) d -> p t d", p=P),
+            )
+
+        q_raw = []
+
+        def load_q(idx):
+            h, nq, g = groups[idx]
+            raw = raw_pool.tile([P, 4096], BF16, tag="raw", name="q_raw%d" % idx)
+            for n in range(NB):
+                rows = q[NB * nq + n, h, 256 * g : 256 * (g + 1), :]
+                nc.sync.dma_start(
+                    out=raw[n:P:NB, :],
+                    in_=rows.rearrange("(a b) d -> a (b d)", b=ROWS),
+                )
+            q_raw.append(raw)
+
+        load_e(0)
+        load_q(0)
+        load_q(1)
+        load_e(1)
+        for idx in range(2, 7):
+            load_q(idx)
+
+        ident = const.tile([P, P], F32, name="ident")
+        make_identity(nc, ident[:])
+        mask = const.tile([P, 256], F32, name="mask")
+        nc.gpsimd.memset(mask[:], 1.0)
+        nc.gpsimd.affine_select(
+            out=mask[:],
+            in_=mask[:],
+            pattern=[[4, 32], [0, 8]],
+            compare_op=IS_GE,
+            fill=0.0,
+            base=-124,
+            channel_multiplier=1,
+        )
+        e_codes = const.tile([P, 1024], U32, name="e_codes", align_bytes=64)
+        e_scales = const.tile([P, 1024], U8, name="e_scales", align_bytes=64)
+
+        out_tiles = []
+        for idx in range(8):
+            ot = out_pool.tile([P, RUN], F32, name="ot%d" % idx)
+            zero_cols = 264 if groups[idx][2] == 0 else 8
+            nc.vector.memset(
+                ot[:, 0 : ROWS * L].rearrange("p (b s) -> p b s", b=ROWS)[:, :, 0:zero_cols], 0.0
+            )
+            out_tiles.append(ot)
+
+        def pack(raw, codes, scales, halves):
+            raw32 = raw[:].bitcast(F32)
+            stage = stage_pool.tile([P, 4096], BF16, tag="stage", align_bytes=64)
+            stage32 = stage[:].bitcast(F32)
+            for hf in halves:
+                for j in (2 * hf, 2 * hf + 1):
+                    xt = psum_t.tile([P, 2, 2, P], F32, tag="xt")
+                    for t in range(2):
+                        for u in range(2):
+                            c0 = 512 * j + 256 * t + 128 * u
+                            nc.tensor.transpose(xt[:, t, u, :], raw32[:, c0 : c0 + 128], ident[:])
+                    nc.scalar.copy(
+                        out=stage32[:, 512 * j : 512 * (j + 1)].rearrange(
+                            "p (t r u) -> p t r u", t=2, u=2
+                        ),
+                        in_=xt[:].rearrange("p t u r -> p t r u"),
+                    )
+                nc.vector.quantize_mx(
+                    out=codes[:, 512 * hf : 512 * (hf + 1)].bitcast(FP8X4),
+                    scales=scales[:, 512 * hf : 512 * (hf + 1)],
+                    in_=stage[:, 2048 * hf : 2048 * (hf + 1)],
+                )
+
+        packed = []
+
+        def pack_q(idx):
+            codes = code_pool.tile([P, 1024], U32, tag="codes", align_bytes=64)
+            scales = code_pool.tile([P, 1024], U8, tag="scales", align_bytes=64)
+            pack(q_raw[idx], codes, scales, (0, 1))
+            packed.append((codes, scales))
+
+        def mx(acc, idx, b, m0, width):
+            h = groups[idx][0]
+            codes, scales = packed[idx]
+            nc.tensor.matmul_mx(
+                out=acc,
+                lhsT=codes[:, P * b : P * (b + 1)].bitcast(FP8X4),
+                lhsT_scale=scales[:, P * b : P * (b + 1)],
+                rhs=e_codes[:, L * h + m0 : L * h + m0 + width].bitcast(FP8X4),
+                rhs_scale=e_scales[:, L * h + m0 : L * h + m0 + width],
+                start=True,
+                stop=True,
+            )
+
+        def multiply(idx):
+            g = groups[idx][2]
+            ot = out_tiles[idx]
+            for b0 in range(0, ROWS, 2):
+                head = psum_m.tile([P, 2, 256], F32, tag="acc")
+                for j in range(2):
+                    mx(head[:, j, :], idx, b0 + j, 256 if g == 0 else 0, 256)
+                fulls = []
+                if g == 1:
+                    for j in range(2):
+                        full = psum_m.tile([P, L], F32, tag="acc")
+                        mx(full[:], idx, b0 + j, 0, L)
+                        fulls.append(full)
+                for j in range(2):
+                    b = b0 + j
+                    if g == 0:
+                        nc.vector.tensor_tensor(
+                            out=ot[:, L * b + 264 : L * b + 513 + b],
+                            in0=head[:, j, 7 - b : 256],
+                            in1=mask[:, 0 : 249 + b],
+                            op=MULT,
+                        )
+                    else:
+                        nc.vector.tensor_tensor(
+                            out=ot[:, L * b + 8 : L * b + 256],
+                            in0=head[:, j, 7 - b : 255 - b],
+                            in1=mask[:, 0:248],
+                            op=MULT,
+                        )
+                        nc.scalar.copy(
+                            out=ot[:, L * b + 256 : L * b + 513 + b],
+                            in_=fulls[j][:, 255 - b : L],
+                        )
+
+        def store(idx):
+            h, nq, g = groups[idx]
+            ot = out_tiles[idx]
+            for n in range(NB):
+                base = ((NB * nq + n) * H + h) * L * L + g * NA * RUN - L
+                if base >= 0:
+                    nc.sync.dma_start(
+                        out=out_flat[base : base + NA * RUN].rearrange("(a s) -> a s", s=RUN),
+                        in_=ot[n:P:NB, :],
+                    )
+                else:
+                    rows = out_flat[0 : NA * RUN].rearrange("(a s) -> a s", s=RUN)
+                    nc.sync.dma_start(out=rows[:, 0 : RUN - L], in_=ot[n:P:NB, L:RUN])
+                    nc.sync.dma_start(
+                        out=rows[0 : NA - 1, RUN - L : RUN], in_=ot[n + NB : P : NB, 0:L]
+                    )
+
+        pack(e_raw, e_codes, e_scales, (0,))
+        pack_q(0)
+        for idx in range(8):
+            if idx == 1:
+                pack(e_raw, e_codes, e_scales, (1,))
+                load_q(7)
+            if idx + 1 < 8:
+                pack_q(idx + 1)
+            multiply(idx)
+            store(idx)

@@ -26,6 +26,7 @@ def tile_subsampledrelativeattention_t_kernel(tc, q, e, out):
     groups = [(h, nq, g) for g in range(2) for h in range(H) for nq in range(2)]
 
     with ExitStack() as ctx:
+        ctx.enter_context(tc.manual_schedule())
         const = ctx.enter_context(tc.tile_pool(name="const", bufs=1))
         raw_pool = ctx.enter_context(tc.tile_pool(name="raw", bufs=8))
         stage_pool = ctx.enter_context(tc.tile_pool(name="stage", bufs=2))
@@ -57,9 +58,8 @@ def tile_subsampledrelativeattention_t_kernel(tc, q, e, out):
 
         load_e(0)
         load_q(0)
-        load_q(1)
         load_e(1)
-        for idx in range(2, 7):
+        for idx in range(1, 7):
             load_q(idx)
 
         ident = const.tile([P, P], F32, name="ident")
@@ -178,16 +178,21 @@ def tile_subsampledrelativeattention_t_kernel(tc, q, e, out):
                 else:
                     rows = out_flat[0 : NA * RUN].rearrange("(a s) -> a s", s=RUN)
                     nc.sync.dma_start(out=rows[:, 0 : RUN - L], in_=ot[n:P:NB, L:RUN])
+                    half = NA // 2
                     nc.sync.dma_start(
-                        out=rows[0 : NA - 1, RUN - L : RUN], in_=ot[n + NB : P : NB, 0:L]
+                        out=rows[0 : half - 1, RUN - L : RUN],
+                        in_=ot[n + NB : n + NB * half : NB, 0:L],
+                    )
+                    nc.sync.dma_start(
+                        out=rows[half - 1 : NA - 1, RUN - L : RUN],
+                        in_=ot[n + NB * half : P : NB, 0:L],
                     )
 
         pack(e_raw, e_codes, e_scales, (0,))
         pack_q(0)
+        pack(e_raw, e_codes, e_scales, (1,))
+        load_q(7)
         for idx in range(8):
-            if idx == 1:
-                pack(e_raw, e_codes, e_scales, (1,))
-                load_q(7)
             if idx + 1 < 8:
                 pack_q(idx + 1)
             multiply(idx)

@@ -39,8 +39,8 @@ def tile_subsampledrelativeattention_t_kernel(tc, q, e, out):
 
         def load_e(h):
             nc.sync.dma_start(
-                out=e_raw[:, 2048 * h : 2048 * (h + 1)].rearrange("p (t d) -> p t d", t=4),
-                in_=e[h].rearrange("(t p) d -> p t d", p=P),
+                out=e_raw[:, 2048 * h : 2048 * (h + 1)],
+                in_=e[h].rearrange("(p t) d -> p (t d)", t=4),
             )
 
         q_raw = []
@@ -48,12 +48,8 @@ def tile_subsampledrelativeattention_t_kernel(tc, q, e, out):
         def load_q(idx):
             h, nq, g = groups[idx]
             raw = raw_pool.tile([P, 4096], BF16, tag="raw", name="q_raw%d" % idx)
-            for n in range(NB):
-                rows = q[NB * nq + n, h, 256 * g : 256 * (g + 1), :]
-                nc.sync.dma_start(
-                    out=raw[n:P:NB, :],
-                    in_=rows.rearrange("(a b) d -> a (b d)", b=ROWS),
-                )
+            rows = q[NB * nq : NB * (nq + 1), h, 256 * g : 256 * (g + 1), :]
+            nc.sync.dma_start(out=raw[:], in_=rows.rearrange("n (a b) d -> a n (b d)", b=ROWS))
             q_raw.append(raw)
 
         load_e(0)
@@ -87,7 +83,7 @@ def tile_subsampledrelativeattention_t_kernel(tc, q, e, out):
             )
             out_tiles.append(ot)
 
-        def pack(raw, codes, scales, halves):
+        def pack(raw, codes, scales, halves, rows_interleaved):
             raw32 = raw[:].bitcast(F32)
             stage = stage_pool.tile([P, 4096], BF16, tag="stage", align_bytes=64)
             stage32 = stage[:].bitcast(F32)
@@ -98,12 +94,20 @@ def tile_subsampledrelativeattention_t_kernel(tc, q, e, out):
                         for u in range(2):
                             c0 = 512 * j + 256 * t + 128 * u
                             nc.tensor.transpose(xt[:, t, u, :], raw32[:, c0 : c0 + 128], ident[:])
-                    nc.scalar.copy(
-                        out=stage32[:, 512 * j : 512 * (j + 1)].rearrange(
-                            "p (t r u) -> p t r u", t=2, u=2
-                        ),
-                        in_=xt[:].rearrange("p t u r -> p t r u"),
-                    )
+                    if rows_interleaved:
+                        nc.scalar.copy(
+                            out=stage32[:, 1024 * hf : 1024 * (hf + 1)].rearrange(
+                                "p (r w x) -> p w r x", w=2, x=4
+                            )[:, j - 2 * hf],
+                            in_=xt[:].rearrange("p t u r -> p r (t u)"),
+                        )
+                    else:
+                        nc.scalar.copy(
+                            out=stage32[:, 512 * j : 512 * (j + 1)].rearrange(
+                                "p (t r u) -> p t r u", t=2, u=2
+                            ),
+                            in_=xt[:].rearrange("p t u r -> p t r u"),
+                        )
                 nc.vector.quantize_mx(
                     out=codes[:, 512 * hf : 512 * (hf + 1)].bitcast(FP8X4),
                     scales=scales[:, 512 * hf : 512 * (hf + 1)],
@@ -115,7 +119,7 @@ def tile_subsampledrelativeattention_t_kernel(tc, q, e, out):
         def pack_q(idx):
             codes = code_pool.tile([P, 1024], U32, tag="codes", align_bytes=64)
             scales = code_pool.tile([P, 1024], U8, tag="scales", align_bytes=64)
-            pack(q_raw[idx], codes, scales, (0, 1))
+            pack(q_raw[idx], codes, scales, (0, 1), False)
             packed.append((codes, scales))
 
         def mx(acc, idx, b, m0, width):
@@ -168,6 +172,20 @@ def tile_subsampledrelativeattention_t_kernel(tc, q, e, out):
         def store(idx):
             h, nq, g = groups[idx]
             ot = out_tiles[idx]
+            pair = H * L * L
+            first = (NB * nq * H + h) * L * L + g * NA * RUN - L
+            if first >= 0:
+                if first % pair + NA * RUN <= pair:
+                    view = out_flat.rearrange("(t r) -> t r", r=pair)
+                    t0, col = first // pair, first % pair
+                else:
+                    view = out_flat[L * L : L * L + (B - 1) * pair].rearrange("(t r) -> t r", r=pair)
+                    t0, col = (first - L * L) // pair, (first - L * L) % pair
+                nc.sync.dma_start(
+                    out=view[t0 : t0 + NB, col : col + NA * RUN].rearrange("n (a s) -> a n s", s=RUN),
+                    in_=ot[:],
+                )
+                return
             for n in range(NB):
                 base = ((NB * nq + n) * H + h) * L * L + g * NA * RUN - L
                 if base >= 0:
@@ -188,9 +206,9 @@ def tile_subsampledrelativeattention_t_kernel(tc, q, e, out):
                         in_=ot[n + NB * half : P : NB, 0:L],
                     )
 
-        pack(e_raw, e_codes, e_scales, (0,))
+        pack(e_raw, e_codes, e_scales, (0,), True)
         pack_q(0)
-        pack(e_raw, e_codes, e_scales, (1,))
+        pack(e_raw, e_codes, e_scales, (1,), True)
         load_q(7)
         for idx in range(8):
             if idx + 1 < 8:

@@ -28,14 +28,14 @@ def tile_subsampledrelativeattention_t_kernel(tc, q, e, out):
     with ExitStack() as ctx:
         ctx.enter_context(tc.manual_schedule())
         const = ctx.enter_context(tc.tile_pool(name="const", bufs=1))
-        raw_pool = ctx.enter_context(tc.tile_pool(name="raw", bufs=8))
+        raw_pool = ctx.enter_context(tc.tile_pool(name="raw", bufs=7))
         stage_pool = ctx.enter_context(tc.tile_pool(name="stage", bufs=2))
-        code_pool = ctx.enter_context(tc.tile_pool(name="code", bufs=3))
+        code_pool = ctx.enter_context(tc.tile_pool(name="code", bufs=2))
         out_pool = ctx.enter_context(tc.tile_pool(name="outp", bufs=1))
-        psum_t = ctx.enter_context(tc.psum_pool(name="psum_t", bufs=3))
-        psum_m = ctx.enter_context(tc.psum_pool(name="psum_m", bufs=5))
+        psum_t = ctx.enter_context(tc.psum_pool(name="psum_t", bufs=4))
+        psum_m = ctx.enter_context(tc.psum_pool(name="psum_m", bufs=4))
 
-        e_raw = raw_pool.tile([P, 4096], BF16, tag="raw", name="e_raw")
+        e_raw = const.tile([P, 4096], BF16, name="e_raw")
 
         def load_e(h):
             nc.sync.dma_start(
@@ -60,26 +60,30 @@ def tile_subsampledrelativeattention_t_kernel(tc, q, e, out):
 
         ident = const.tile([P, P], F32, name="ident")
         make_identity(nc, ident[:])
-        mask = const.tile([P, 256], F32, name="mask")
-        nc.gpsimd.memset(mask[:], 1.0)
+        stair = const.tile([P, 264], F32, name="stair")
+        nc.gpsimd.memset(stair[:], 1.0)
         nc.gpsimd.affine_select(
-            out=mask[:],
-            in_=mask[:],
-            pattern=[[4, 32], [0, 8]],
+            out=stair[:],
+            in_=stair[:],
+            pattern=[[4, 33], [0, 8]],
             compare_op=IS_GE,
             fill=0.0,
-            base=-124,
+            base=-128,
             channel_multiplier=1,
         )
+        mask = const.tile([P, ROWS, 256], F32, name="mask")
+        for b in range(ROWS):
+            nc.scalar.copy(out=mask[:, b, :], in_=stair[:, b + 1 : b + 257])
         e_codes = const.tile([P, 1024], U32, name="e_codes", align_bytes=64)
         e_scales = const.tile([P, 1024], U8, name="e_scales", align_bytes=64)
 
         out_tiles = []
-        for idx in range(8):
+
+        def clear(idx):
             ot = out_pool.tile([P, RUN], F32, name="ot%d" % idx)
-            zero_cols = 264 if groups[idx][2] == 0 else 8
+            zero_cols = 257 - 256 * groups[idx][2]
             nc.vector.memset(
-                ot[:, 0 : ROWS * L].rearrange("p (b s) -> p b s", b=ROWS)[:, :, 0:zero_cols], 0.0
+                ot[:].rearrange("p (b s) -> p b s", b=ROWS)[:, :, 0:zero_cols], 0.0
             )
             out_tiles.append(ot)
 
@@ -138,36 +142,24 @@ def tile_subsampledrelativeattention_t_kernel(tc, q, e, out):
         def multiply(idx):
             g = groups[idx][2]
             ot = out_tiles[idx]
+            rows = ot[:].rearrange("p (b s) -> p b s", b=ROWS)
+            m0 = 256 if g == 0 else 0
             for b0 in range(0, ROWS, 2):
                 head = psum_m.tile([P, 2, 256], F32, tag="acc")
                 for j in range(2):
-                    mx(head[:, j, :], idx, b0 + j, 256 if g == 0 else 0, 256)
-                fulls = []
+                    mx(head[:, j, :], idx, b0 + j, m0, 256)
                 if g == 1:
+                    tail = psum_m.tile([P, 2, 256], F32, tag="acc")
                     for j in range(2):
-                        full = psum_m.tile([P, L], F32, tag="acc")
-                        mx(full[:], idx, b0 + j, 0, L)
-                        fulls.append(full)
-                for j in range(2):
-                    b = b0 + j
-                    if g == 0:
-                        nc.vector.tensor_tensor(
-                            out=ot[:, L * b + 264 : L * b + 513 + b],
-                            in0=head[:, j, 7 - b : 256],
-                            in1=mask[:, 0 : 249 + b],
-                            op=MULT,
-                        )
-                    else:
-                        nc.vector.tensor_tensor(
-                            out=ot[:, L * b + 8 : L * b + 256],
-                            in0=head[:, j, 7 - b : 255 - b],
-                            in1=mask[:, 0:248],
-                            op=MULT,
-                        )
-                        nc.scalar.copy(
-                            out=ot[:, L * b + 256 : L * b + 513 + b],
-                            in_=fulls[j][:, 255 - b : L],
-                        )
+                        mx(tail[:, j, :], idx, b0 + j, 256, 256)
+                nc.vector.tensor_tensor(
+                    out=rows[:, b0 : b0 + 2, m0 + 1 : m0 + 257],
+                    in0=head[:],
+                    in1=mask[:, b0 : b0 + 2, :],
+                    op=MULT,
+                )
+                if g == 1:
+                    nc.scalar.copy(out=rows[:, b0 : b0 + 2, 257:513], in_=tail[:])
 
         def store(idx):
             h, nq, g = groups[idx]
@@ -206,6 +198,8 @@ def tile_subsampledrelativeattention_t_kernel(tc, q, e, out):
                         in_=ot[n + NB * half : P : NB, 0:L],
                     )
 
+        for idx in range(4):
+            clear(idx)
         pack(e_raw, e_codes, e_scales, (0,), True)
         pack_q(0)
         pack(e_raw, e_codes, e_scales, (1,), True)
@@ -213,5 +207,7 @@ def tile_subsampledrelativeattention_t_kernel(tc, q, e, out):
         for idx in range(8):
             if idx + 1 < 8:
                 pack_q(idx + 1)
+            if idx + 4 < 8:
+                clear(idx + 4)
             multiply(idx)
             store(idx)

@@ -35,27 +35,25 @@ def tile_subsampledrelativeattention_t_kernel(tc, q, e, out):
         psum_t = ctx.enter_context(tc.psum_pool(name="psum_t", bufs=4))
         psum_m = ctx.enter_context(tc.psum_pool(name="psum_m", bufs=4))
 
-        e_raw = const.tile([P, 4096], BF16, name="e_raw")
+        e_raw = const.tile([P, 4096], BF16, name="e_raw", align_bytes=256)
 
-        def load_e(h):
-            nc.sync.dma_start(
-                out=e_raw[:, 2048 * h : 2048 * (h + 1)],
-                in_=e[h].rearrange("(p t) d -> p (t d)", t=4),
-            )
+        nc.sync.dma_start(
+            out=e_raw[:],
+            in_=e.rearrange("h m d -> (h m) d").rearrange("(p t) d -> p (t d)", t=8),
+        )
 
         q_raw = []
 
         def load_q(idx):
             h, nq, g = groups[idx]
-            raw = raw_pool.tile([P, 4096], BF16, tag="raw", name="q_raw%d" % idx)
+            raw = raw_pool.tile(
+                [P, 4096], BF16, tag="raw", name="q_raw%d" % idx, align_bytes=256
+            )
             rows = q[NB * nq : NB * (nq + 1), h, 256 * g : 256 * (g + 1), :]
             nc.sync.dma_start(out=raw[:], in_=rows.rearrange("n (a b) d -> a n (b d)", b=ROWS))
             q_raw.append(raw)
 
-        load_e(0)
-        load_q(0)
-        load_e(1)
-        for idx in range(1, 7):
+        for idx in range(7):
             load_q(idx)
 
         ident = const.tile([P, P], F32, name="ident")
@@ -80,50 +78,56 @@ def tile_subsampledrelativeattention_t_kernel(tc, q, e, out):
         out_tiles = []
 
         def clear(idx):
-            ot = out_pool.tile([P, RUN], F32, name="ot%d" % idx)
+            ot = out_pool.tile([P, RUN], F32, name="ot%d" % idx, align_bytes=256)
             zero_cols = 257 - 256 * groups[idx][2]
             nc.vector.memset(
                 ot[:].rearrange("p (b s) -> p b s", b=ROWS)[:, :, 0:zero_cols], 0.0
             )
             out_tiles.append(ot)
 
-        def pack(raw, codes, scales, halves, rows_interleaved):
-            raw32 = raw[:].bitcast(F32)
+        def transpose_rows(raw32, j):
+            xt = psum_t.tile([P, 2, 2, P], F32, tag="xt")
+            for t in range(2):
+                for u in range(2):
+                    c0 = 512 * j + 256 * t + 128 * u
+                    nc.tensor.transpose(xt[:, t, u, :], raw32[:, c0 : c0 + 128], ident[:])
+            return xt
+
+        def quantize_half(codes, scales, stage, hf):
+            nc.vector.quantize_mx(
+                out=codes[:, 512 * hf : 512 * (hf + 1)].bitcast(FP8X4),
+                scales=scales[:, 512 * hf : 512 * (hf + 1)],
+                in_=stage[:, 2048 * hf : 2048 * (hf + 1)],
+            )
+
+        def pack_e():
+            raw32 = e_raw[:].bitcast(F32)
             stage = stage_pool.tile([P, 4096], BF16, tag="stage", align_bytes=64)
-            stage32 = stage[:].bitcast(F32)
-            for hf in halves:
-                for j in (2 * hf, 2 * hf + 1):
-                    xt = psum_t.tile([P, 2, 2, P], F32, tag="xt")
-                    for t in range(2):
-                        for u in range(2):
-                            c0 = 512 * j + 256 * t + 128 * u
-                            nc.tensor.transpose(xt[:, t, u, :], raw32[:, c0 : c0 + 128], ident[:])
-                    if rows_interleaved:
-                        nc.scalar.copy(
-                            out=stage32[:, 1024 * hf : 1024 * (hf + 1)].rearrange(
-                                "p (r w x) -> p w r x", w=2, x=4
-                            )[:, j - 2 * hf],
-                            in_=xt[:].rearrange("p t u r -> p r (t u)"),
-                        )
-                    else:
-                        nc.scalar.copy(
-                            out=stage32[:, 512 * j : 512 * (j + 1)].rearrange(
-                                "p (t r u) -> p t r u", t=2, u=2
-                            ),
-                            in_=xt[:].rearrange("p t u r -> p t r u"),
-                        )
-                nc.vector.quantize_mx(
-                    out=codes[:, 512 * hf : 512 * (hf + 1)].bitcast(FP8X4),
-                    scales=scales[:, 512 * hf : 512 * (hf + 1)],
-                    in_=stage[:, 2048 * hf : 2048 * (hf + 1)],
-                )
+            by_pair = stage[:].bitcast(F32).rearrange("p (r w x) -> p w r x", w=4, x=4)
+            for j in range(4):
+                xt = transpose_rows(raw32, j)
+                nc.scalar.copy(out=by_pair[:, j], in_=xt[:].rearrange("p t u r -> p r (t u)"))
+            for hf in range(2):
+                quantize_half(e_codes, e_scales, stage, hf)
 
         packed = []
 
         def pack_q(idx):
             codes = code_pool.tile([P, 1024], U32, tag="codes", align_bytes=64)
             scales = code_pool.tile([P, 1024], U8, tag="scales", align_bytes=64)
-            pack(q_raw[idx], codes, scales, (0, 1), False)
+            raw32 = q_raw[idx][:].bitcast(F32)
+            stage = stage_pool.tile([P, 4096], BF16, tag="stage", align_bytes=64)
+            stage32 = stage[:].bitcast(F32)
+            for j in range(4):
+                xt = transpose_rows(raw32, j)
+                nc.scalar.copy(
+                    out=stage32[:, 512 * j : 512 * (j + 1)].rearrange(
+                        "p (t r u) -> p t r u", t=2, u=2
+                    ),
+                    in_=xt[:].rearrange("p t u r -> p t r u"),
+                )
+                if j % 2 == 1:
+                    quantize_half(codes, scales, stage, j // 2)
             packed.append((codes, scales))
 
         def mx(acc, idx, b, m0, width):
@@ -200,9 +204,8 @@ def tile_subsampledrelativeattention_t_kernel(tc, q, e, out):
 
         for idx in range(4):
             clear(idx)
-        pack(e_raw, e_codes, e_scales, (0,), True)
+        pack_e()
         pack_q(0)
-        pack(e_raw, e_codes, e_scales, (1,), True)
         load_q(7)
         for idx in range(8):
             if idx + 1 < 8:

@@ -112,12 +112,13 @@ def tile_subsampledrelativeattention_t_kernel(tc, q, e, out):
 
         packed = []
 
-        def pack_q(idx):
+        def pack_q(idx, between=None):
             codes = code_pool.tile([P, 1024], U32, tag="codes", align_bytes=64)
             scales = code_pool.tile([P, 1024], U8, tag="scales", align_bytes=64)
             raw32 = q_raw[idx][:].bitcast(F32)
             stage = stage_pool.tile([P, 4096], BF16, tag="stage", align_bytes=64)
             stage32 = stage[:].bitcast(F32)
+            packed.append((codes, scales))
             for j in range(4):
                 xt = transpose_rows(raw32, j)
                 nc.scalar.copy(
@@ -126,9 +127,10 @@ def tile_subsampledrelativeattention_t_kernel(tc, q, e, out):
                     ),
                     in_=xt[:].rearrange("p t u r -> p t r u"),
                 )
+                if j == 1 and between is not None:
+                    between()
                 if j % 2 == 1:
                     quantize_half(codes, scales, stage, j // 2)
-            packed.append((codes, scales))
 
         def mx(acc, idx, b, m0, width):
             h = groups[idx][0]
@@ -202,15 +204,20 @@ def tile_subsampledrelativeattention_t_kernel(tc, q, e, out):
                         in_=ot[n + NB * half : P : NB, 0:L],
                     )
 
-        for idx in range(4):
+        for idx in range(3):
             clear(idx)
         pack_e()
         pack_q(0)
         load_q(7)
-        for idx in range(8):
+        multiply(0)
+        clear(3)
+        store(0)
+        pack_q(1)
+        for idx in range(1, 8):
+            if idx >= 4:
+                clear(idx)
             if idx + 1 < 8:
-                pack_q(idx + 1)
-            if idx + 4 < 8:
-                clear(idx + 4)
-            multiply(idx)
+                pack_q(idx + 1, lambda: multiply(idx))
+            else:
+                multiply(idx)
             store(idx)

from contextlib import ExitStack

import concourse.mybir as mybir
from concourse.masks import make_identity

F32 = mybir.dt.float32
BF16 = mybir.dt.bfloat16
U32 = mybir.dt.uint32
U8 = mybir.dt.uint8
FP8X4 = mybir.dt.float8_e4m3fn_x4
MULT = mybir.AluOpType.mult
IS_GE = mybir.AluOpType.is_ge

B, H, L, D = 8, 2, 512, 512
P = 128
ROWS = 8
RUN = ROWS * (L + 1)
NB = 4
NA = P // NB
FLOPS = 2 * B * H * L * L * D


def tile_subsampledrelativeattention_t_kernel(tc, q, e, out):
    nc = tc.nc
    out_flat = out.rearrange("b h i j -> (b h i j)")
    groups = [(h, nq, g) for g in range(2) for h in range(H) for nq in range(2)]

    with ExitStack() as ctx:
        ctx.enter_context(tc.manual_schedule())
        const = ctx.enter_context(tc.tile_pool(name="const", bufs=1))
        raw_pool = ctx.enter_context(tc.tile_pool(name="raw", bufs=7))
        stage_pool = ctx.enter_context(tc.tile_pool(name="stage", bufs=2))
        code_pool = ctx.enter_context(tc.tile_pool(name="code", bufs=2))
        out_pool = ctx.enter_context(tc.tile_pool(name="outp", bufs=1))
        psum_t = ctx.enter_context(tc.psum_pool(name="psum_t", bufs=4))
        psum_m = ctx.enter_context(tc.psum_pool(name="psum_m", bufs=4))

        e_raw = const.tile([P, 4096], BF16, name="e_raw", align_bytes=256)

        nc.sync.dma_start(
            out=e_raw[:],
            in_=e.rearrange("h m d -> (h m) d").rearrange("(p t) d -> p (t d)", t=8),
        )

        q_raw = []

        def load_q(idx):
            h, nq, g = groups[idx]
            raw = raw_pool.tile(
                [P, 4096], BF16, tag="raw", name="q_raw%d" % idx, align_bytes=256
            )
            rows = q[NB * nq : NB * (nq + 1), h, 256 * g : 256 * (g + 1), :]
            nc.sync.dma_start(out=raw[:], in_=rows.rearrange("n (a b) d -> a n (b d)", b=ROWS))
            q_raw.append(raw)

        for idx in range(7):
            load_q(idx)

        ident = const.tile([P, P], F32, name="ident")
        make_identity(nc, ident[:])
        stair = const.tile([P, 264], F32, name="stair")
        nc.gpsimd.memset(stair[:], 1.0)
        nc.gpsimd.affine_select(
            out=stair[:],
            in_=stair[:],
            pattern=[[4, 33], [0, 8]],
            compare_op=IS_GE,
            fill=0.0,
            base=-128,
            channel_multiplier=1,
        )
        mask = const.tile([P, ROWS, 256], F32, name="mask")
        for b in range(ROWS):
            nc.scalar.copy(out=mask[:, b, :], in_=stair[:, b + 1 : b + 257])
        e_codes = const.tile([P, 1024], U32, name="e_codes", align_bytes=64)
        e_scales = const.tile([P, 1024], U8, name="e_scales", align_bytes=64)

        out_tiles = []

        def clear(idx):
            ot = out_pool.tile([P, RUN], F32, name="ot%d" % idx, align_bytes=256)
            zero_cols = 257 - 256 * groups[idx][2]
            nc.vector.memset(
                ot[:].rearrange("p (b s) -> p b s", b=ROWS)[:, :, 0:zero_cols], 0.0
            )
            out_tiles.append(ot)

        def transpose_rows(raw32, j):
            xt = psum_t.tile([P, 2, 2, P], F32, tag="xt")
            for t in range(2):
                for u in range(2):
                    c0 = 512 * j + 256 * t + 128 * u
                    nc.tensor.transpose(xt[:, t, u, :], raw32[:, c0 : c0 + 128], ident[:])
            return xt

        def quantize_half(codes, scales, stage, hf):
            nc.vector.quantize_mx(
                out=codes[:, 512 * hf : 512 * (hf + 1)].bitcast(FP8X4),
                scales=scales[:, 512 * hf : 512 * (hf + 1)],
                in_=stage[:, 2048 * hf : 2048 * (hf + 1)],
            )

        def pack_e():
            raw32 = e_raw[:].bitcast(F32)
            stage = stage_pool.tile([P, 4096], BF16, tag="stage", align_bytes=64)
            by_pair = stage[:].bitcast(F32).rearrange("p (r w x) -> p w r x", w=4, x=4)
            for j in range(4):
                xt = transpose_rows(raw32, j)
                nc.scalar.copy(out=by_pair[:, j], in_=xt[:].rearrange("p t u r -> p r (t u)"))
            for hf in range(2):
                quantize_half(e_codes, e_scales, stage, hf)

        packed = []

        def pack_q(idx, between=None):
            codes = code_pool.tile([P, 1024], U32, tag="codes", align_bytes=64)
            scales = code_pool.tile([P, 1024], U8, tag="scales", align_bytes=64)
            raw32 = q_raw[idx][:].bitcast(F32)
            stage = stage_pool.tile([P, 4096], BF16, tag="stage", align_bytes=64)
            stage32 = stage[:].bitcast(F32)
            packed.append((codes, scales))
            for j in range(4):
                xt = transpose_rows(raw32, j)
                nc.scalar.copy(
                    out=stage32[:, 512 * j : 512 * (j + 1)].rearrange(
                        "p (t r u) -> p t r u", t=2, u=2
                    ),
                    in_=xt[:].rearrange("p t u r -> p t r u"),
                )
                if j == 1 and between is not None:
                    between()
                if j % 2 == 1:
                    quantize_half(codes, scales, stage, j // 2)

        def mx(acc, idx, b, m0, width):
            h = groups[idx][0]
            codes, scales = packed[idx]
            nc.tensor.matmul_mx(
                out=acc,
                lhsT=codes[:, P * b : P * (b + 1)].bitcast(FP8X4),
                lhsT_scale=scales[:, P * b : P * (b + 1)],
                rhs=e_codes[:, L * h + m0 : L * h + m0 + width].bitcast(FP8X4),
                rhs_scale=e_scales[:, L * h + m0 : L * h + m0 + width],
                start=True,
                stop=True,
            )

        def multiply(idx):
            g = groups[idx][2]
            ot = out_tiles[idx]
            rows = ot[:].rearrange("p (b s) -> p b s", b=ROWS)
            m0 = 256 if g == 0 else 0
            for b0 in range(0, ROWS, 2):
                head = psum_m.tile([P, 2, 256], F32, tag="acc")
                for j in range(2):
                    mx(head[:, j, :], idx, b0 + j, m0, 256)
                if g == 1:
                    tail = psum_m.tile([P, 2, 256], F32, tag="acc")
                    for j in range(2):
                        mx(tail[:, j, :], idx, b0 + j, 256, 256)
                nc.vector.tensor_tensor(
                    out=rows[:, b0 : b0 + 2, m0 + 1 : m0 + 257],
                    in0=head[:],
                    in1=mask[:, b0 : b0 + 2, :],
                    op=MULT,
                )
                if g == 1:
                    nc.scalar.copy(out=rows[:, b0 : b0 + 2, 257:513], in_=tail[:])

        def store(idx):
            h, nq, g = groups[idx]
            ot = out_tiles[idx]
            pair = H * L * L
            first = (NB * nq * H + h) * L * L + g * NA * RUN - L
            if first >= 0:
                if first % pair + NA * RUN <= pair:
                    view = out_flat.rearrange("(t r) -> t r", r=pair)
                    t0, col = first // pair, first % pair
                else:
                    view = out_flat[L * L : L * L + (B - 1) * pair].rearrange("(t r) -> t r", r=pair)
                    t0, col = (first - L * L) // pair, (first - L * L) % pair
                nc.sync.dma_start(
                    out=view[t0 : t0 + NB, col : col + NA * RUN].rearrange("n (a s) -> a n s", s=RUN),
                    in_=ot[:],
                )
                return
            for n in range(NB):
                base = ((NB * nq + n) * H + h) * L * L + g * NA * RUN - L
                if base >= 0:
                    nc.sync.dma_start(
                        out=out_flat[base : base + NA * RUN].rearrange("(a s) -> a s", s=RUN),
                        in_=ot[n:P:NB, :],
                    )
                else:
                    rows = out_flat[0 : NA * RUN].rearrange("(a s) -> a s", s=RUN)
                    nc.sync.dma_start(out=rows[:, 0 : RUN - L], in_=ot[n:P:NB, L:RUN])
                    half = NA // 2
                    nc.sync.dma_start(
                        out=rows[0 : half - 1, RUN - L : RUN],
                        in_=ot[n + NB : n + NB * half : NB, 0:L],
                    )
                    nc.sync.dma_start(
                        out=rows[half - 1 : NA - 1, RUN - L : RUN],
                        in_=ot[n + NB * half : P : NB, 0:L],
                    )

        for idx in range(3):
            clear(idx)
        pack_e()
        pack_q(0)
        load_q(7)
        multiply(0)
        clear(3)
        store(0)
        pack_q(1)
        for idx in range(1, 8):
            if idx >= 4:
                clear(idx)
            if idx + 1 < 8:
                pack_q(idx + 1, lambda: multiply(idx))
            else:
                multiply(idx)
            store(idx)
